import numpy as np
import ml_dtypes

BF16 = ml_dtypes.bfloat16


def bf(x):
    return np.asarray(x, np.float32).astype(BF16)


def f32(x):
    return np.asarray(x, np.float32)


def f64(x):
    return np.asarray(x).astype(np.float64)


def striped(idx):
    return np.tile(idx.reshape(-1, 16).T, (8, 1))


S, D, M, N = 1024, 128, 128, 256


def setup_inputs():
    return {"table": bf(np.random.standard_normal((S, D))), "w": bf(np.random.standard_normal((D, M)) / np.sqrt(D)), "w_dense": bf(np.random.standard_normal((M, M)) / np.sqrt(M)), "offs": striped(np.random.permutation(S)[:N])}


def reference(table, w, w_dense, offs):
    idx = offs[:16].T.reshape(-1)
    v = f64(w).T @ f64(table)[idx].T
    return f64(w_dense).T @ v

@@ -1,0 +1,50 @@
+import concourse.mybir as mybir
+from concourse.masks import make_identity
+
+P = 128
+S = 1024
+N = 256
+BLOCKS = S // P
+
+BF16, F32, U16 = mybir.dt.bfloat16, mybir.dt.float32, mybir.dt.uint16
+
+FLOPS = 2 * (2 * P * P * N)
+
+
+def tile_cogvlmvisionexpertattention_kernel(tc, table, w, w_dense, offs, out):
+    nc = tc.nc
+    with (
+        tc.tile_pool(name="held", bufs=1) as held,
+        tc.psum_pool(name="psum", bufs=1) as psum,
+    ):
+        offsets = held.tile([P, N // 16], U16, name="offsets")
+        nc.sync.dma_start(offsets[:], offs)
+
+        tokens = held.tile([P, BLOCKS, P], BF16, name="tokens")
+        nc.sync.dma_start(tokens[:], table.rearrange("(b p) d -> p b d", p=P))
+
+        value_w = held.tile([P, P], BF16, name="value_w")
+        nc.scalar.dma_start(value_w[:], w)
+        dense_w = held.tile([P, P], BF16, name="dense_w")
+        nc.scalar.dma_start(dense_w[:], w_dense)
+
+        identity = held.tile([P, P], BF16, name="identity")
+        make_identity(nc, identity[:])
+
+        flipped = psum.tile([P, S], BF16, name="flipped")
+        for b in range(BLOCKS):
+            nc.tensor.transpose(flipped[:, b * P : (b + 1) * P], tokens[:, b, :], identity[:])
+
+        window = held.tile([P, S], BF16, name="window")
+        nc.vector.tensor_copy(window[:], flipped[:])
+
+        v_acc = psum.tile([P, N], F32, name="v_acc")
+        nc.tensor.matmul(v_acc[:], value_w[:], window[:].indirect(offsets[:]), start=True, stop=True)
+        v = held.tile([P, N], BF16, name="v")
+        nc.vector.tensor_copy(v[:], v_acc[:])
+
+        out_acc = psum.tile([P, N], F32, name="out_acc")
+        nc.tensor.matmul(out_acc[:], dense_w[:], v[:], start=True, stop=True)
+        result = held.tile([P, N], F32, name="result")
+        nc.vector.tensor_copy(result[:], out_acc[:])
+        nc.sync.dma_start(out, result[:])

@@ -4,7 +4,9 @@ from concourse.masks import make_identity
 P = 128
 S = 1024
 N = 256
-BLOCKS = S // P
+CHUNKS = 4
+CHUNK = S // CHUNKS
+BLOCKS = CHUNK // P
 
 BF16, F32, U16 = mybir.dt.bfloat16, mybir.dt.float32, mybir.dt.uint16
 
@@ -17,26 +19,31 @@ def tile_cogvlmvisionexpertattention_kernel(tc, table, w, w_dense, offs, out):
         tc.tile_pool(name="held", bufs=1) as held,
         tc.psum_pool(name="psum", bufs=1) as psum,
     ):
+        tokens = held.tile([P, CHUNKS, BLOCKS, P], BF16, name="tokens")
+        chunked = table.rearrange("(c b p) d -> c p b d", c=CHUNKS, p=P)
+        for c in range(CHUNKS):
+            queue = nc.sync if c % 2 == 0 else nc.scalar
+            queue.dma_start(tokens[:, c], chunked[c])
+
         offsets = held.tile([P, N // 16], U16, name="offsets")
         nc.sync.dma_start(offsets[:], offs)
-
-        tokens = held.tile([P, BLOCKS, P], BF16, name="tokens")
-        nc.sync.dma_start(tokens[:], table.rearrange("(b p) d -> p b d", p=P))
-
         value_w = held.tile([P, P], BF16, name="value_w")
-        nc.scalar.dma_start(value_w[:], w)
+        nc.sync.dma_start(value_w[:], w)
         dense_w = held.tile([P, P], BF16, name="dense_w")
         nc.scalar.dma_start(dense_w[:], w_dense)
 
         identity = held.tile([P, P], BF16, name="identity")
         make_identity(nc, identity[:])
 
-        flipped = psum.tile([P, S], BF16, name="flipped")
-        for b in range(BLOCKS):
-            nc.tensor.transpose(flipped[:, b * P : (b + 1) * P], tokens[:, b, :], identity[:])
-
         window = held.tile([P, S], BF16, name="window")
-        nc.vector.tensor_copy(window[:], flipped[:])
+        for c in range(CHUNKS):
+            flipped = psum.tile([P, CHUNK], BF16, name=f"flipped{c}")
+            for b in range(BLOCKS):
+                nc.tensor.transpose(flipped[:, b * P : (b + 1) * P], tokens[:, c, b, :], identity[:])
+            if c % 2 == 0:
+                nc.vector.tensor_copy(window[:, c * CHUNK : (c + 1) * CHUNK], flipped[:])
+            else:
+                nc.scalar.copy(window[:, c * CHUNK : (c + 1) * CHUNK], flipped[:])
 
         v_acc = psum.tile([P, N], F32, name="v_acc")
         nc.tensor.matmul(v_acc[:], value_w[:], window[:].indirect(offsets[:]), start=True, stop=True)

@@ -7,6 +7,8 @@ N = 256
 CHUNKS = 4
 CHUNK = S // CHUNKS
 BLOCKS = CHUNK // P
+PIECES = 2
+PIECE = N // PIECES
 
 BF16, F32, U16 = mybir.dt.bfloat16, mybir.dt.float32, mybir.dt.uint16
 
@@ -45,13 +47,18 @@ def tile_cogvlmvisionexpertattention_kernel(tc, table, w, w_dense, offs, out):
             else:
                 nc.scalar.copy(window[:, c * CHUNK : (c + 1) * CHUNK], flipped[:])
 
-        v_acc = psum.tile([P, N], F32, name="v_acc")
-        nc.tensor.matmul(v_acc[:], value_w[:], window[:].indirect(offsets[:]), start=True, stop=True)
-        v = held.tile([P, N], BF16, name="v")
-        nc.vector.tensor_copy(v[:], v_acc[:])
+        v = []
+        for i in range(PIECES):
+            piece_offsets = offsets[:, i * (PIECE // 16) : (i + 1) * (PIECE // 16)]
+            v_acc = psum.tile([P, PIECE], F32, name=f"v_acc{i}")
+            nc.tensor.matmul(v_acc[:], value_w[:], window[:].indirect(piece_offsets), start=True, stop=True)
+            v.append(held.tile([P, PIECE], BF16, name=f"v{i}"))
+            nc.vector.tensor_copy(v[i][:], v_acc[:])
 
-        out_acc = psum.tile([P, N], F32, name="out_acc")
-        nc.tensor.matmul(out_acc[:], dense_w[:], v[:], start=True, stop=True)
-        result = held.tile([P, N], F32, name="result")
-        nc.vector.tensor_copy(result[:], out_acc[:])
-        nc.sync.dma_start(out, result[:])
+        for i in range(PIECES):
+            out_acc = psum.tile([P, PIECE], F32, name=f"out_acc{i}")
+            nc.tensor.matmul(out_acc[:], dense_w[:], v[i][:], start=True, stop=True)
+            result = held.tile([P, PIECE], F32, name=f"result{i}")
+            nc.vector.tensor_copy(result[:], out_acc[:])
+            queue = nc.sync if i % 2 == 0 else nc.scalar
+            queue.dma_start(out[:, i * PIECE : (i + 1) * PIECE], result[:])

@@ -7,8 +7,8 @@ N = 256
 CHUNKS = 4
 CHUNK = S // CHUNKS
 BLOCKS = CHUNK // P
-PIECES = 2
-PIECE = N // PIECES
+WARM_COLUMNS = 512
+WARM_MATMULS = 5
 
 BF16, F32, U16 = mybir.dt.bfloat16, mybir.dt.float32, mybir.dt.uint16
 
@@ -37,6 +37,12 @@ def tile_cogvlmvisionexpertattention_kernel(tc, table, w, w_dense, offs, out):
         identity = held.tile([P, P], BF16, name="identity")
         make_identity(nc, identity[:])
 
+        zeros = held.tile([P, WARM_COLUMNS], BF16, name="zeros")
+        nc.vector.memset(zeros[:], 0.0)
+        warm_acc = psum.tile([P, WARM_COLUMNS], F32, name="warm_acc")
+        for k in range(WARM_MATMULS):
+            nc.tensor.matmul(warm_acc[:], zeros[:, 0:P], zeros[:], start=True, stop=True)
+
         window = held.tile([P, S], BF16, name="window")
         for c in range(CHUNKS):
             flipped = psum.tile([P, CHUNK], BF16, name=f"flipped{c}")
@@ -47,18 +53,13 @@ def tile_cogvlmvisionexpertattention_kernel(tc, table, w, w_dense, offs, out):
             else:
                 nc.scalar.copy(window[:, c * CHUNK : (c + 1) * CHUNK], flipped[:])
 
-        v = []
-        for i in range(PIECES):
-            piece_offsets = offsets[:, i * (PIECE // 16) : (i + 1) * (PIECE // 16)]
-            v_acc = psum.tile([P, PIECE], F32, name=f"v_acc{i}")
-            nc.tensor.matmul(v_acc[:], value_w[:], window[:].indirect(piece_offsets), start=True, stop=True)
-            v.append(held.tile([P, PIECE], BF16, name=f"v{i}"))
-            nc.vector.tensor_copy(v[i][:], v_acc[:])
+        v_acc = psum.tile([P, N], F32, name="v_acc")
+        nc.tensor.matmul(v_acc[:], value_w[:], window[:].indirect(offsets[:]), start=True, stop=True)
+        v = held.tile([P, N], BF16, name="v")
+        nc.vector.tensor_copy(v[:], v_acc[:])
 
-        for i in range(PIECES):
-            out_acc = psum.tile([P, PIECE], F32, name=f"out_acc{i}")
-            nc.tensor.matmul(out_acc[:], dense_w[:], v[i][:], start=True, stop=True)
-            result = held.tile([P, PIECE], F32, name=f"result{i}")
-            nc.vector.tensor_copy(result[:], out_acc[:])
-            queue = nc.sync if i % 2 == 0 else nc.scalar
-            queue.dma_start(out[:, i * PIECE : (i + 1) * PIECE], result[:])
+        out_acc = psum.tile([P, N], F32, name="out_acc")
+        nc.tensor.matmul(out_acc[:], dense_w[:], v[:], start=True, stop=True)
+        result = held.tile([P, N], F32, name="result")
+        nc.vector.tensor_copy(result[:], out_acc[:])
+        nc.sync.dma_start(out, result[:])

@@ -7,8 +7,6 @@ N = 256
 CHUNKS = 4
 CHUNK = S // CHUNKS
 BLOCKS = CHUNK // P
-WARM_COLUMNS = 512
-WARM_MATMULS = 5
 
 BF16, F32, U16 = mybir.dt.bfloat16, mybir.dt.float32, mybir.dt.uint16
 
@@ -37,21 +35,12 @@ def tile_cogvlmvisionexpertattention_kernel(tc, table, w, w_dense, offs, out):
         identity = held.tile([P, P], BF16, name="identity")
         make_identity(nc, identity[:])
 
-        zeros = held.tile([P, WARM_COLUMNS], BF16, name="zeros")
-        nc.vector.memset(zeros[:], 0.0)
-        warm_acc = psum.tile([P, WARM_COLUMNS], F32, name="warm_acc")
-        for k in range(WARM_MATMULS):
-            nc.tensor.matmul(warm_acc[:], zeros[:, 0:P], zeros[:], start=True, stop=True)
-
         window = held.tile([P, S], BF16, name="window")
         for c in range(CHUNKS):
             flipped = psum.tile([P, CHUNK], BF16, name=f"flipped{c}")
             for b in range(BLOCKS):
                 nc.tensor.transpose(flipped[:, b * P : (b + 1) * P], tokens[:, c, b, :], identity[:])
-            if c % 2 == 0:
-                nc.vector.tensor_copy(window[:, c * CHUNK : (c + 1) * CHUNK], flipped[:])
-            else:
-                nc.scalar.copy(window[:, c * CHUNK : (c + 1) * CHUNK], flipped[:])
+            nc.vector.tensor_copy(window[:, c * CHUNK : (c + 1) * CHUNK], flipped[:])
 
         v_acc = psum.tile([P, N], F32, name="v_acc")
         nc.tensor.matmul(v_acc[:], value_w[:], window[:].indirect(offsets[:]), start=True, stop=True)

@@ -4,9 +4,7 @@ from concourse.masks import make_identity
 P = 128
 S = 1024
 N = 256
-CHUNKS = 4
-CHUNK = S // CHUNKS
-BLOCKS = CHUNK // P
+BLOCKS = S // P
 
 BF16, F32, U16 = mybir.dt.bfloat16, mybir.dt.float32, mybir.dt.uint16
 
@@ -17,13 +15,13 @@ def tile_cogvlmvisionexpertattention_kernel(tc, table, w, w_dense, offs, out):
     nc = tc.nc
     with (
         tc.tile_pool(name="held", bufs=1) as held,
-        tc.psum_pool(name="psum", bufs=1) as psum,
+        tc.psum_pool(name="flip", bufs=4) as flip,
+        tc.psum_pool(name="acc", bufs=1) as acc,
     ):
-        tokens = held.tile([P, CHUNKS, BLOCKS, P], BF16, name="tokens")
-        chunked = table.rearrange("(c b p) d -> c p b d", c=CHUNKS, p=P)
-        for c in range(CHUNKS):
-            queue = nc.sync if c % 2 == 0 else nc.scalar
-            queue.dma_start(tokens[:, c], chunked[c])
+        tokens = held.tile([P, BLOCKS, P], BF16, name="tokens")
+        for b in range(BLOCKS):
+            queue = nc.sync if b % 2 == 0 else nc.scalar
+            queue.dma_start(tokens[:, b, :], table[b * P : (b + 1) * P, :])
 
         offsets = held.tile([P, N // 16], U16, name="offsets")
         nc.sync.dma_start(offsets[:], offs)
@@ -36,18 +34,17 @@ def tile_cogvlmvisionexpertattention_kernel(tc, table, w, w_dense, offs, out):
         make_identity(nc, identity[:])
 
         window = held.tile([P, S], BF16, name="window")
-        for c in range(CHUNKS):
-            flipped = psum.tile([P, CHUNK], BF16, name=f"flipped{c}")
-            for b in range(BLOCKS):
-                nc.tensor.transpose(flipped[:, b * P : (b + 1) * P], tokens[:, c, b, :], identity[:])
-            nc.vector.tensor_copy(window[:, c * CHUNK : (c + 1) * CHUNK], flipped[:])
+        for b in range(BLOCKS):
+            flipped = flip.tile([P, P], BF16, name="flipped")
+            nc.tensor.transpose(flipped[:], tokens[:, b, :], identity[:])
+            nc.vector.tensor_copy(window[:, b * P : (b + 1) * P], flipped[:])
 
-        v_acc = psum.tile([P, N], F32, name="v_acc")
+        v_acc = acc.tile([P, N], F32, name="v_acc")
         nc.tensor.matmul(v_acc[:], value_w[:], window[:].indirect(offsets[:]), start=True, stop=True)
         v = held.tile([P, N], BF16, name="v")
         nc.vector.tensor_copy(v[:], v_acc[:])
 
-        out_acc = psum.tile([P, N], F32, name="out_acc")
+        out_acc = acc.tile([P, N], F32, name="out_acc")
         nc.tensor.matmul(out_acc[:], dense_w[:], v[:], start=True, stop=True)
         result = held.tile([P, N], F32, name="result")
         nc.vector.tensor_copy(result[:], out_acc[:])

@@ -4,7 +4,9 @@ from concourse.masks import make_identity
 P = 128
 S = 1024
 N = 256
-BLOCKS = S // P
+CHUNKS = 4
+CHUNK = S // CHUNKS
+BLOCKS = CHUNK // P
 
 BF16, F32, U16 = mybir.dt.bfloat16, mybir.dt.float32, mybir.dt.uint16
 
@@ -15,13 +17,13 @@ def tile_cogvlmvisionexpertattention_kernel(tc, table, w, w_dense, offs, out):
     nc = tc.nc
     with (
         tc.tile_pool(name="held", bufs=1) as held,
-        tc.psum_pool(name="flip", bufs=4) as flip,
-        tc.psum_pool(name="acc", bufs=1) as acc,
+        tc.psum_pool(name="psum", bufs=1) as psum,
     ):
-        tokens = held.tile([P, BLOCKS, P], BF16, name="tokens")
-        for b in range(BLOCKS):
-            queue = nc.sync if b % 2 == 0 else nc.scalar
-            queue.dma_start(tokens[:, b, :], table[b * P : (b + 1) * P, :])
+        tokens = held.tile([P, CHUNKS, BLOCKS, P], BF16, name="tokens")
+        chunked = table.rearrange("(c b p) d -> c p b d", c=CHUNKS, p=P)
+        for c in range(CHUNKS):
+            queue = nc.sync if c % 2 == 0 else nc.scalar
+            queue.dma_start(tokens[:, c], chunked[c])
 
         offsets = held.tile([P, N // 16], U16, name="offsets")
         nc.sync.dma_start(offsets[:], offs)
@@ -34,18 +36,20 @@ def tile_cogvlmvisionexpertattention_kernel(tc, table, w, w_dense, offs, out):
         make_identity(nc, identity[:])
 
         window = held.tile([P, S], BF16, name="window")
-        for b in range(BLOCKS):
-            flipped = flip.tile([P, P], BF16, name="flipped")
-            nc.tensor.transpose(flipped[:], tokens[:, b, :], identity[:])
-            nc.vector.tensor_copy(window[:, b * P : (b + 1) * P], flipped[:])
+        for c in range(CHUNKS):
+            flipped = psum.tile([P, CHUNK], BF16, name=f"flipped{c}")
+            for b in range(BLOCKS):
+                nc.tensor.transpose(flipped[:, b * P : (b + 1) * P], tokens[:, c, b, :], identity[:])
+            nc.vector.tensor_copy(window[:, c * CHUNK : (c + 1) * CHUNK], flipped[:])
 
-        v_acc = acc.tile([P, N], F32, name="v_acc")
+        v_acc = psum.tile([P, N], F32, name="v_acc")
         nc.tensor.matmul(v_acc[:], value_w[:], window[:].indirect(offsets[:]), start=True, stop=True)
         v = held.tile([P, N], BF16, name="v")
         nc.vector.tensor_copy(v[:], v_acc[:])
 
-        out_acc = acc.tile([P, N], F32, name="out_acc")
+        out_acc = psum.tile([P, N], F32, name="out_acc")
         nc.tensor.matmul(out_acc[:], dense_w[:], v[:], start=True, stop=True)
         result = held.tile([P, N], F32, name="result")
         nc.vector.tensor_copy(result[:], out_acc[:])
-        nc.sync.dma_start(out, result[:])
+        nc.sync.dma_start(out[:, 0 : N // 2], result[:, 0 : N // 2])
+        nc.scalar.dma_start(out[:, N // 2 : N], result[:, N // 2 : N])

@@ -3,14 +3,21 @@ from concourse.masks import make_identity
 
 P = 128
 S = 1024
+D = 128
+M = 128
 N = 256
+
 CHUNKS = 4
 CHUNK = S // CHUNKS
 BLOCKS = CHUNK // P
 
+PIECES = 2
+PIECE = N // PIECES
+PIECE_COLUMNS = PIECE // 16
+
 BF16, F32, U16 = mybir.dt.bfloat16, mybir.dt.float32, mybir.dt.uint16
 
-FLOPS = 2 * (2 * P * P * N)
+FLOPS = 2 * D * M * N + 2 * M * M * N
 
 
 def tile_cogvlmvisionexpertattention_kernel(tc, table, w, w_dense, offs, out):
@@ -19,7 +26,7 @@ def tile_cogvlmvisionexpertattention_kernel(tc, table, w, w_dense, offs, out):
         tc.tile_pool(name="held", bufs=1) as held,
         tc.psum_pool(name="psum", bufs=1) as psum,
     ):
-        tokens = held.tile([P, CHUNKS, BLOCKS, P], BF16, name="tokens")
+        tokens = held.tile([P, CHUNKS, BLOCKS, D], BF16, name="tokens")
         chunked = table.rearrange("(c b p) d -> c p b d", c=CHUNKS, p=P)
         for c in range(CHUNKS):
             queue = nc.sync if c % 2 == 0 else nc.scalar
@@ -27,29 +34,31 @@ def tile_cogvlmvisionexpertattention_kernel(tc, table, w, w_dense, offs, out):
 
         offsets = held.tile([P, N // 16], U16, name="offsets")
         nc.sync.dma_start(offsets[:], offs)
-        value_w = held.tile([P, P], BF16, name="value_w")
+        value_w = held.tile([D, M], BF16, name="value_w")
         nc.sync.dma_start(value_w[:], w)
-        dense_w = held.tile([P, P], BF16, name="dense_w")
+        dense_w = held.tile([M, M], BF16, name="dense_w")
         nc.scalar.dma_start(dense_w[:], w_dense)
 
         identity = held.tile([P, P], BF16, name="identity")
         make_identity(nc, identity[:])
 
-        window = held.tile([P, S], BF16, name="window")
+        window = held.tile([D, S], BF16, name="window")
         for c in range(CHUNKS):
-            flipped = psum.tile([P, CHUNK], BF16, name=f"flipped{c}")
+            flipped = psum.tile([D, CHUNK], BF16, name=f"flipped{c}")
             for b in range(BLOCKS):
                 nc.tensor.transpose(flipped[:, b * P : (b + 1) * P], tokens[:, c, b, :], identity[:])
             nc.vector.tensor_copy(window[:, c * CHUNK : (c + 1) * CHUNK], flipped[:])
 
-        v_acc = psum.tile([P, N], F32, name="v_acc")
-        nc.tensor.matmul(v_acc[:], value_w[:], window[:].indirect(offsets[:]), start=True, stop=True)
-        v = held.tile([P, N], BF16, name="v")
-        nc.vector.tensor_copy(v[:], v_acc[:])
+        v = held.tile([M, N], BF16, name="v")
+        for i in range(PIECES):
+            piece_offsets = offsets[:, i * PIECE_COLUMNS : (i + 1) * PIECE_COLUMNS]
+            v_acc = psum.tile([M, PIECE], F32, name=f"v_acc{i}")
+            nc.tensor.matmul(v_acc[:], value_w[:], window[:].indirect(piece_offsets), start=True, stop=True)
+            nc.vector.tensor_copy(v[:, i * PIECE : (i + 1) * PIECE], v_acc[:])
 
-        out_acc = psum.tile([P, N], F32, name="out_acc")
-        nc.tensor.matmul(out_acc[:], dense_w[:], v[:], start=True, stop=True)
-        result = held.tile([P, N], F32, name="result")
-        nc.vector.tensor_copy(result[:], out_acc[:])
-        nc.sync.dma_start(out[:, 0 : N // 2], result[:, 0 : N // 2])
-        nc.scalar.dma_start(out[:, N // 2 : N], result[:, N // 2 : N])
+        result = held.tile([M, N], F32, name="result")
+        for i in range(PIECES):
+            out_acc = psum.tile([M, PIECE], F32, name=f"out_acc{i}")
+            nc.tensor.matmul(out_acc[:], dense_w[:], v[:, i * PIECE : (i + 1) * PIECE], start=True, stop=True)
+            nc.vector.tensor_copy(result[:, i * PIECE : (i + 1) * PIECE], out_acc[:])
+        nc.sync.dma_start(out, result[:])

@@ -29,15 +29,14 @@ def tile_cogvlmvisionexpertattention_kernel(tc, table, w, w_dense, offs, out):
         tokens = held.tile([P, CHUNKS, BLOCKS, D], BF16, name="tokens")
         chunked = table.rearrange("(c b p) d -> c p b d", c=CHUNKS, p=P)
         for c in range(CHUNKS):
-            queue = nc.sync if c % 2 == 0 else nc.scalar
-            queue.dma_start(tokens[:, c], chunked[c])
+            nc.sync.dma_start(tokens[:, c], chunked[c])
 
         offsets = held.tile([P, N // 16], U16, name="offsets")
         nc.sync.dma_start(offsets[:], offs)
         value_w = held.tile([D, M], BF16, name="value_w")
         nc.sync.dma_start(value_w[:], w)
         dense_w = held.tile([M, M], BF16, name="dense_w")
-        nc.scalar.dma_start(dense_w[:], w_dense)
+        nc.sync.dma_start(dense_w[:], w_dense)
 
         identity = held.tile([P, P], BF16, name="identity")
         make_identity(nc, identity[:])

@@ -11,9 +11,8 @@ CHUNKS = 4
 CHUNK = S // CHUNKS
 BLOCKS = CHUNK // P
 
-PIECES = 2
-PIECE = N // PIECES
-PIECE_COLUMNS = PIECE // 16
+PIECE_COLUMNS = (6, 6, 4)
+assert 16 * sum(PIECE_COLUMNS) == N
 
 BF16, F32, U16 = mybir.dt.bfloat16, mybir.dt.float32, mybir.dt.uint16
 
@@ -49,15 +48,21 @@ def tile_cogvlmvisionexpertattention_kernel(tc, table, w, w_dense, offs, out):
             nc.vector.tensor_copy(window[:, c * CHUNK : (c + 1) * CHUNK], flipped[:])
 
         v = held.tile([M, N], BF16, name="v")
-        for i in range(PIECES):
-            piece_offsets = offsets[:, i * PIECE_COLUMNS : (i + 1) * PIECE_COLUMNS]
-            v_acc = psum.tile([M, PIECE], F32, name=f"v_acc{i}")
+        column = 0
+        for i, columns in enumerate(PIECE_COLUMNS):
+            picked = slice(16 * column, 16 * (column + columns))
+            v_acc = psum.tile([M, 16 * columns], F32, name=f"v_acc{i}")
+            piece_offsets = offsets[:, column : column + columns]
             nc.tensor.matmul(v_acc[:], value_w[:], window[:].indirect(piece_offsets), start=True, stop=True)
-            nc.vector.tensor_copy(v[:, i * PIECE : (i + 1) * PIECE], v_acc[:])
+            nc.vector.tensor_copy(v[:, picked], v_acc[:])
+            column += columns
 
         result = held.tile([M, N], F32, name="result")
-        for i in range(PIECES):
-            out_acc = psum.tile([M, PIECE], F32, name=f"out_acc{i}")
-            nc.tensor.matmul(out_acc[:], dense_w[:], v[:, i * PIECE : (i + 1) * PIECE], start=True, stop=True)
-            nc.vector.tensor_copy(result[:, i * PIECE : (i + 1) * PIECE], out_acc[:])
+        column = 0
+        for i, columns in enumerate(PIECE_COLUMNS):
+            picked = slice(16 * column, 16 * (column + columns))
+            out_acc = psum.tile([M, 16 * columns], F32, name=f"out_acc{i}", tag=f"flipped{i}")
+            nc.tensor.matmul(out_acc[:], dense_w[:], v[:, picked], start=True, stop=True)
+            nc.vector.tensor_copy(result[:, picked], out_acc[:])
+            column += columns
         nc.sync.dma_start(out, result[:])

@@ -8,8 +8,10 @@ M = 128
 N = 256
 
 CHUNKS = 4
-CHUNK = S // CHUNKS
-BLOCKS = CHUNK // P
+BLOCKS = S // CHUNKS // P
+
+GROUP_BLOCKS = (2, 2, 2, 1, 1)
+assert sum(GROUP_BLOCKS) == CHUNKS * BLOCKS
 
 PIECE_COLUMNS = (6, 6, 4)
 assert 16 * sum(PIECE_COLUMNS) == N
@@ -41,11 +43,14 @@ def tile_cogvlmvisionexpertattention_kernel(tc, table, w, w_dense, offs, out):
         make_identity(nc, identity[:])
 
         window = held.tile([D, S], BF16, name="window")
-        for c in range(CHUNKS):
-            flipped = psum.tile([D, CHUNK], BF16, name=f"flipped{c}")
-            for b in range(BLOCKS):
-                nc.tensor.transpose(flipped[:, b * P : (b + 1) * P], tokens[:, c, b, :], identity[:])
-            nc.vector.tensor_copy(window[:, c * CHUNK : (c + 1) * CHUNK], flipped[:])
+        first = 0
+        for g, blocks in enumerate(GROUP_BLOCKS):
+            flipped = psum.tile([D, blocks * P], BF16, name=f"flipped{g}")
+            for k in range(blocks):
+                c, b = divmod(first + k, BLOCKS)
+                nc.tensor.transpose(flipped[:, k * P : (k + 1) * P], tokens[:, c, b, :], identity[:])
+            nc.vector.tensor_copy(window[:, first * P : (first + blocks) * P], flipped[:])
+            first += blocks
 
         v = held.tile([M, N], BF16, name="v")
         column = 0

@@ -9,9 +9,12 @@ N = 256
 
 CHUNKS = 4
 BLOCKS = S // CHUNKS // P
+CHUNK = BLOCKS * P
 
-GROUP_BLOCKS = (2, 2, 2, 1, 1)
-assert sum(GROUP_BLOCKS) == CHUNKS * BLOCKS
+PAIRED_CHUNKS = 1
+
+GROUP_BLOCKS = (2, 2, 1, 1)
+assert sum(GROUP_BLOCKS) == (CHUNKS - PAIRED_CHUNKS) * BLOCKS
 
 PIECE_COLUMNS = (6, 6, 4)
 assert 16 * sum(PIECE_COLUMNS) == N
@@ -28,9 +31,10 @@ def tile_cogvlmvisionexpertattention_kernel(tc, table, w, w_dense, offs, out):
         tc.psum_pool(name="psum", bufs=1) as psum,
     ):
         tokens = held.tile([P, CHUNKS, BLOCKS, D], BF16, name="tokens")
-        chunked = table.rearrange("(c b p) d -> c p b d", c=CHUNKS, p=P)
+        paired = table.rearrange("(c p b) d -> c p b d", c=CHUNKS, p=P)
+        plain = table.rearrange("(c b p) d -> c p b d", c=CHUNKS, p=P)
         for c in range(CHUNKS):
-            nc.sync.dma_start(tokens[:, c], chunked[c])
+            nc.sync.dma_start(tokens[:, c], paired[c] if c < PAIRED_CHUNKS else plain[c])
 
         offsets = held.tile([P, N // 16], U16, name="offsets")
         nc.sync.dma_start(offsets[:], offs)
@@ -43,7 +47,16 @@ def tile_cogvlmvisionexpertattention_kernel(tc, table, w, w_dense, offs, out):
         make_identity(nc, identity[:])
 
         window = held.tile([D, S], BF16, name="window")
-        first = 0
+
+        for c in range(PAIRED_CHUNKS):
+            flipped = psum.tile([D, CHUNK], BF16, name=f"paired{c}")
+            for b in range(BLOCKS):
+                nc.tensor.transpose(flipped[:, b * P : (b + 1) * P], tokens[:, c, b, :], identity[:])
+            in_order = flipped[:].rearrange("d (b p) -> d p b", b=BLOCKS)
+            ordered = window[:, c * CHUNK : (c + 1) * CHUNK].rearrange("d (p b) -> d p b", b=BLOCKS)
+            nc.vector.tensor_copy(ordered, in_order)
+
+        first = PAIRED_CHUNKS * BLOCKS
         for g, blocks in enumerate(GROUP_BLOCKS):
             flipped = psum.tile([D, blocks * P], BF16, name=f"flipped{g}")
             for k in range(blocks):

import concourse.mybir as mybir
from concourse.masks import make_identity

P = 128
S = 1024
D = 128
M = 128
N = 256

CHUNKS = 4
BLOCKS = S // CHUNKS // P
CHUNK = BLOCKS * P

PAIRED_CHUNKS = 1

GROUP_BLOCKS = (2, 2, 1, 1)
assert sum(GROUP_BLOCKS) == (CHUNKS - PAIRED_CHUNKS) * BLOCKS

PIECE_COLUMNS = (6, 6, 4)
assert 16 * sum(PIECE_COLUMNS) == N

BF16, F32, U16 = mybir.dt.bfloat16, mybir.dt.float32, mybir.dt.uint16

FLOPS = 2 * D * M * N + 2 * M * M * N


def tile_cogvlmvisionexpertattention_kernel(tc, table, w, w_dense, offs, out):
    nc = tc.nc
    with (
        tc.tile_pool(name="held", bufs=1) as held,
        tc.psum_pool(name="psum", bufs=1) as psum,
    ):
        tokens = held.tile([P, CHUNKS, BLOCKS, D], BF16, name="tokens")
        paired = table.rearrange("(c p b) d -> c p b d", c=CHUNKS, p=P)
        plain = table.rearrange("(c b p) d -> c p b d", c=CHUNKS, p=P)
        for c in range(CHUNKS):
            nc.sync.dma_start(tokens[:, c], paired[c] if c < PAIRED_CHUNKS else plain[c])

        offsets = held.tile([P, N // 16], U16, name="offsets")
        nc.sync.dma_start(offsets[:], offs)
        value_w = held.tile([D, M], BF16, name="value_w")
        nc.sync.dma_start(value_w[:], w)
        dense_w = held.tile([M, M], BF16, name="dense_w")
        nc.sync.dma_start(dense_w[:], w_dense)

        identity = held.tile([P, P], BF16, name="identity")
        make_identity(nc, identity[:])

        window = held.tile([D, S], BF16, name="window")

        for c in range(PAIRED_CHUNKS):
            flipped = psum.tile([D, CHUNK], BF16, name=f"paired{c}")
            for b in range(BLOCKS):
                nc.tensor.transpose(flipped[:, b * P : (b + 1) * P], tokens[:, c, b, :], identity[:])
            in_order = flipped[:].rearrange("d (b p) -> d p b", b=BLOCKS)
            ordered = window[:, c * CHUNK : (c + 1) * CHUNK].rearrange("d (p b) -> d p b", b=BLOCKS)
            nc.vector.tensor_copy(ordered, in_order)

        first = PAIRED_CHUNKS * BLOCKS
        for g, blocks in enumerate(GROUP_BLOCKS):
            flipped = psum.tile([D, blocks * P], BF16, name=f"flipped{g}")
            for k in range(blocks):
                c, b = divmod(first + k, BLOCKS)
                nc.tensor.transpose(flipped[:, k * P : (k + 1) * P], tokens[:, c, b, :], identity[:])
            nc.vector.tensor_copy(window[:, first * P : (first + blocks) * P], flipped[:])
            first += blocks

        v = held.tile([M, N], BF16, name="v")
        column = 0
        for i, columns in enumerate(PIECE_COLUMNS):
            picked = slice(16 * column, 16 * (column + columns))
            v_acc = psum.tile([M, 16 * columns], F32, name=f"v_acc{i}")
            piece_offsets = offsets[:, column : column + columns]
            nc.tensor.matmul(v_acc[:], value_w[:], window[:].indirect(piece_offsets), start=True, stop=True)
            nc.vector.tensor_copy(v[:, picked], v_acc[:])
            column += columns

        result = held.tile([M, N], F32, name="result")
        column = 0
        for i, columns in enumerate(PIECE_COLUMNS):
            picked = slice(16 * column, 16 * (column + columns))
            out_acc = psum.tile([M, 16 * columns], F32, name=f"out_acc{i}", tag=f"flipped{i}")
            nc.tensor.matmul(out_acc[:], dense_w[:], v[:, picked], start=True, stop=True)
            nc.vector.tensor_copy(result[:, picked], out_acc[:])
            column += columns
        nc.sync.dma_start(out, result[:])
